import numpy as np
import ml_dtypes


def mxq(x, axis, fmt="e4m3"):
    dtype, down = {"e4m3": (ml_dtypes.float8_e4m3fn, 7), "e5m2": (ml_dtypes.float8_e5m2, 14)}[fmt]
    v = np.moveaxis(np.asarray(x, np.float32).astype(ml_dtypes.bfloat16).astype(np.float64), axis, -1)
    blocks = v.reshape(v.shape[:-1] + (-1, 32))
    amax = np.abs(blocks).max(-1, keepdims=True)
    byte = np.maximum(np.where(amax > 0, np.frexp(amax)[1] - 1 + 127, 0) - down, 1)
    scale = np.exp2(byte - 127.0)
    codes = (blocks / scale).astype(np.float32).astype(dtype).astype(np.float64)
    return np.moveaxis((codes * scale).reshape(v.shape), -1, axis)


WIDE = False


def mx_kscale(k):
    if not WIDE:
        return np.ones(k)
    levels = np.array([10, -10, 5, -5, 0])
    a = np.random.permutation(np.resize(levels, k // 512 * 4)).reshape(k // 512, 4)
    idx = np.arange(k)
    return np.exp2(a[idx // 512, idx % 128 // 32])


BF16 = ml_dtypes.bfloat16


def bf(x):
    return np.asarray(x, np.float32).astype(BF16)


def f64(x):
    return np.asarray(x).astype(np.float64)


B, C, H, W, O, KH, KW, PH, PW, T, R = 4, 1024, 7, 7, 512, 2, 2, 1, 1, 8, 64
HO, WO = H + PH + PH - KH + 1, W + PW + PW - KW + 1
N = B * HO * WO
D = C * KH * KW
R2 = R * KH * KW
K1, K2 = T * R, T * R2


def setup_inputs():
    s, t1, t2 = mx_kscale(D), mx_kscale(K1).reshape(T, R), mx_kscale(K2).reshape(T, R2)
    return {"xw": bf(np.random.standard_normal((N, D)) * s),
            "S1s": bf(np.random.standard_normal((T, D, R)) / np.sqrt(D) / s[None, :, None] * t1[:, None, :]),
            "U1s": bf(np.random.standard_normal((T, R, O)) * T / np.sqrt(K1) / t1[:, :, None]),
            "U2s": bf(np.random.standard_normal((T, R2, D)) / np.sqrt(D) / s[None, None, :] * t2[:, :, None]),
            "S2s": bf(np.random.standard_normal((T, R2, O)) * T / np.sqrt(K2) / t2[:, :, None]),
            "bias": bf(np.random.standard_normal(O) * 0.3)}


def reference(xw, S1s, U1s, U2s, S2s, bias):
    xq = mxq(f64(xw), 1, "e4m3")
    s1 = f64(S1s).transpose(1, 0, 2).reshape(D, K1)
    h1 = xq @ mxq(s1, 0, "e4m3")
    out1 = (mxq(h1, 1, "e4m3") @ mxq(f64(U1s).reshape(K1, O), 0, "e4m3")) / T + f64(bias)
    u2 = f64(U2s).reshape(K2, D)
    h2 = xq @ mxq(u2, 1, "e4m3").T
    out2 = (mxq(h2, 1, "e4m3") @ mxq(f64(S2s).reshape(K2, O), 0, "e4m3")) / T
    out = out1 + out2 + f64(bias)
    return out.reshape(B, HO, WO, O).transpose(0, 3, 1, 2)

@@ -1,0 +1,287 @@
+from contextlib import ExitStack
+
+import concourse.mybir as mybir
+from concourse.masks import make_identity
+
+PIN = True
+
+FLOPS = 2 * 256 * 4096 * (512 + 2048) + 2 * 256 * 512 * (512 + 2048)
+
+BF16 = mybir.dt.bfloat16
+F32 = mybir.dt.float32
+U32 = mybir.dt.uint32
+U8 = mybir.dt.uint8
+FP8X4 = mybir.dt.float8_e4m3fn_x4
+ACT = mybir.ActivationFunctionType
+ALU = mybir.AluOpType
+
+P = 128
+NW = 256
+D = 4096
+NC = 8
+HALF = 2048
+
+
+def tile_skconv2d_pa_kernel(tc, xw, S1s, U1s, U2s, S2s, bias, out):
+    nc = tc.nc
+    u2v = U2s.rearrange("t r k -> (t r) k").rearrange("(g p j) k -> p g j k", p=P, j=4)
+    s1v = S1s.rearrange("t (a p e) r -> p t a (e r)", a=16, p=P, e=2)
+    u1v = U1s.rearrange("t r o -> (t r) o").rearrange("(j p) o -> p j o", p=P)
+    s2v = S2s.rearrange("t r o -> (t r) o").rearrange("(g p j) o -> p g j o", p=P, j=4)
+    outv = out.rearrange("b (q p) i j -> p q b (i j)", p=P)
+
+    with ExitStack() as ctx:
+        const = ctx.enter_context(tc.tile_pool(name="const", bufs=1))
+        rawp = ctx.enter_context(tc.tile_pool(name="rawp", bufs=8))
+        grpp = ctx.enter_context(tc.tile_pool(name="grpp", bufs=3))
+        codp = ctx.enter_context(tc.tile_pool(name="codp", bufs=3))
+        s1gp = ctx.enter_context(tc.tile_pool(name="s1gp", bufs=2))
+        s1cp = ctx.enter_context(tc.tile_pool(name="s1cp", bufs=4))
+        wgp = ctx.enter_context(tc.tile_pool(name="wgp", bufs=2))
+        hgp = ctx.enter_context(tc.tile_pool(name="hgp", bufs=2))
+        tps = ctx.enter_context(tc.psum_pool(name="tps", bufs=6))
+        hps = ctx.enter_context(tc.psum_pool(name="hps", bufs=2))
+        if PIN:
+            ctx.enter_context(tc.manual_schedule())
+
+        ident_f = const.tile([P, P], F32, name="ident_f")
+        make_identity(nc, ident_f[:])
+        ident_b = const.tile([P, P], BF16, name="ident_b")
+        make_identity(nc, ident_b[:])
+        bz = const.tile([P, P], BF16, name="bz")
+        nc.vector.memset(bz[:], 0.0)
+        nc.scalar.dma_start(out=bz[0:4, :], in_=bias.rearrange("(a c) -> a c", a=4))
+
+        xq = const.tile([P, NC, NW], U32, name="xq", align_bytes=64)
+        xs = const.tile([P, NC, NW], U8, name="xs", align_bytes=64)
+        s2r = const.tile([P, 4, 4, 512], BF16, name="s2r")
+        u1r = const.tile([P, 4, 512], BF16, name="u1r")
+        wc = const.tile([P, 5, 512], U32, name="wc", align_bytes=64)
+        ws = const.tile([P, 5, 512], U8, name="ws", align_bytes=64)
+        hqc = const.tile([P, 5, NW], U32, name="hqc", align_bytes=64)
+        hqs = const.tile([P, 5, NW], U8, name="hqs", align_bytes=64)
+        osb = const.tile([P, 4, NW], F32, name="osb")
+        b2 = const.tile([P, 4], F32, name="b2")
+
+        xr = [rawp.tile([P, D], BF16, name="xr%d" % a, tag="raw") for a in range(2)]
+        for hf in range(2):
+            for a in range(2):
+                nc.sync.dma_start(
+                    out=xr[a][:, HALF * hf : HALF * (hf + 1)],
+                    in_=xw[P * a : P * (a + 1), HALF * hf : HALF * (hf + 1)],
+                )
+        u2raw = {}
+        s1raw = {}
+
+        def load_raw(n):
+            if n < 16:
+                t = rawp.tile([P, D], BF16, name="u2r", tag="raw")
+                nc.sync.dma_start(out=t[:], in_=u2v[:, n // 4, n % 4, :])
+                u2raw[n] = t
+            elif n < 20:
+                m = n - 16
+                t = rawp.tile([P, D], BF16, name="s1r", tag="raw")
+                for t2 in range(2):
+                    nc.sync.dma_start(
+                        out=t[:, HALF * t2 : HALF * (t2 + 1)].rearrange("p (a x) -> p a x", a=16),
+                        in_=s1v[:, 2 * m + t2],
+                    )
+                s1raw[m] = t
+            if n == 3:
+                nc.sync.dma_start(out=u1r[:], in_=u1v)
+            if n in (5, 7, 9, 11):
+                g = (n - 5) // 2
+                nc.sync.dma_start(out=s2r[:, g], in_=s2v[:, g])
+
+        for n in range(6):
+            load_raw(n)
+
+        def quant(codes, scales, src):
+            nc.vector.quantize_mx(out=codes.bitcast(FP8X4), scales=scales, in_=src)
+
+        xg = []
+
+        def quant_x(k):
+            quant(
+                xq[:, 2 * k : 2 * k + 2, :].rearrange("p c n -> p (c n)"),
+                xs[:, 2 * k : 2 * k + 2, :].rearrange("p c n -> p (c n)"),
+                xg[k // 2][:, 2 * (k % 2) : 2 * (k % 2) + 2].rearrange("p c n t -> p (c n t)"),
+            )
+
+        for c in range(NC):
+            if c % 4 == 0:
+                xg.append(grpp.tile([P, 4, NW, 4], BF16, name="xg", tag="grp", align_bytes=64))
+            gf = xg[c // 4][:].bitcast(F32)
+            bank = tps.tile([P, 2, NW], F32, name="xb", tag="T")
+            for u in range(2):
+                for a in range(2):
+                    col = 256 * c + P * u
+                    nc.tensor.transpose(
+                        bank[:, u, P * a : P * (a + 1)],
+                        xr[a][:].bitcast(F32)[:, col : col + P],
+                        ident_f[:],
+                    )
+            src = bank[:].rearrange("p u n -> p n u")
+            if c % 2 == 0:
+                nc.vector.tensor_copy(out=gf[:, c % 4], in_=src)
+            else:
+                nc.scalar.copy(out=gf[:, c % 4], in_=src)
+            if c % 2 == 0 and c >= 2:
+                quant_x(c // 2 - 1)
+        quant_x(3)
+        load_raw(6)
+        load_raw(7)
+
+        bt = tps.tile([P, P], BF16, name="bt", tag="T")
+        nc.tensor.transpose(bt[:], bz[:], ident_b[:])
+        nc.scalar.mul(b2[:], bt[:, 0:4], 2.0)
+
+        u2grp = {}
+        u2cod = {}
+        hbank = {}
+        hgrp = {}
+
+        def transposes(i):
+            grp = grpp.tile([P, NC, P, 4], BF16, name="u2g", tag="grp", align_bytes=64)
+            u2grp[i] = grp
+            gf = grp[:].bitcast(F32)
+            rf = u2raw[i][:].bitcast(F32)
+            for b in range(4):
+                bank = tps.tile([P, 2, 2, P], F32, name="ub", tag="T")
+                for c2 in range(2):
+                    for u in range(2):
+                        col = 256 * (2 * b + c2) + P * u
+                        nc.tensor.transpose(bank[:, c2, u, :], rf[:, col : col + P], ident_f[:])
+                src = bank[:].rearrange("p c u r -> p c r u")
+                if b == 0 and i % 2 == 1:
+                    nc.vector.tensor_copy(out=gf[:, 2 * b : 2 * b + 2], in_=src)
+                else:
+                    nc.scalar.copy(out=gf[:, 2 * b : 2 * b + 2], in_=src)
+            load_raw(8 + i)
+
+        def quant_u2(i):
+            cod = codp.tile([P, NC, P], U32, name="u2c", tag="u2c", align_bytes=64)
+            scl = codp.tile([P, NC, P], U8, name="u2s", tag="u2s", align_bytes=64)
+            u2cod[i] = (cod, scl)
+            for hf in range(2):
+                sl = slice(4 * hf, 4 * hf + 4)
+                quant(
+                    cod[:, sl, :].rearrange("p c r -> p (c r)"),
+                    scl[:, sl, :].rearrange("p c r -> p (c r)"),
+                    u2grp[i][:, sl].rearrange("p c r t -> p (c r t)"),
+                )
+
+        def first_stage(key, half, cod, scl):
+            if half == 0:
+                hbank[key] = hps.tile([P, 2, NW], F32, name="hb", tag="h")
+            hb = hbank[key]
+            for c in range(NC):
+                nc.tensor.matmul_mx(
+                    out=hb[:, half, :],
+                    lhsT=cod[:, c, :].bitcast(FP8X4),
+                    lhsT_scale=scl[:, c, :],
+                    rhs=xq[:, c, :].bitcast(FP8X4),
+                    rhs_scale=xs[:, c, :],
+                    start=(c == 0),
+                    stop=(c == NC - 1),
+                )
+
+        def h_copy(s, pair, key):
+            if pair == 0:
+                hgrp[s] = hgp.tile([P, NW, 4], BF16, name="hg", tag="hg", align_bytes=64)
+            nc.scalar.copy(
+                out=hgrp[s][:, :, 2 * pair : 2 * pair + 2],
+                in_=hbank[key][:].rearrange("p j n -> p n j"),
+            )
+
+        def h_quant(s):
+            quant(hqc[:, s, :], hqs[:, s, :], hgrp[s][:].rearrange("p n t -> p (n t)"))
+
+        wgrp = {}
+
+        def w_regroup(s):
+            wg = wgp.tile([P, 512, 4], BF16, name="wg", tag="wg", align_bytes=64)
+            wgrp[s] = wg
+            src = u1r[:] if s == 4 else s2r[:, s]
+            nc.vector.tensor_copy(
+                out=wg[:].rearrange("p (c i) t -> p c t i", i=4),
+                in_=src.rearrange("p t (c i) -> p c t i", i=4),
+            )
+
+        def w_quant(s):
+            quant(wc[:, s, :], ws[:, s, :], wgrp[s][:].rearrange("p o t -> p (o t)"))
+
+        w_order = {4: 4, 6: 0, 8: 1, 10: 2, 12: 3}
+
+        transposes(0)
+        quant_u2(0)
+        transposes(1)
+        quant_u2(1)
+        for i in range(16):
+            g, j = i // 4, i % 4
+            first_stage(("u2", i // 2), j % 2, u2cod[i][0], u2cod[i][1])
+            if i + 2 < 16:
+                transposes(i + 2)
+            if j % 2 == 1:
+                h_copy(g, j // 2, ("u2", i // 2))
+            if i + 2 < 16:
+                quant_u2(i + 2)
+            if j == 3:
+                h_quant(g)
+            if i in w_order:
+                w_regroup(w_order[i])
+            if i - 1 in w_order:
+                w_quant(w_order[i - 1])
+
+        acc = [tps.tile([P, 512], F32, name="acc%d" % q, tag="T") for q in range(4)]
+
+        def second_stage(s, start, stop):
+            for q in range(4):
+                nc.tensor.matmul_mx(
+                    out=acc[q][:, 0:NW],
+                    lhsT=wc[:, s, P * q : P * (q + 1)].bitcast(FP8X4),
+                    lhsT_scale=ws[:, s, P * q : P * (q + 1)],
+                    rhs=hqc[:, s, :].bitcast(FP8X4),
+                    rhs_scale=hqs[:, s, :],
+                    start=start,
+                    stop=stop,
+                )
+
+        for g in range(4):
+            second_stage(g, g == 0, False)
+
+        for m in range(4):
+            s1g = s1gp.tile([P, NC, 2, 64, 4], BF16, name="s1g", tag="s1g", align_bytes=64)
+            cod = s1cp.tile([P, NC, P], U32, name="s1c", tag="s1c", align_bytes=64)
+            scl = s1cp.tile([P, NC, P], U8, name="s1s", tag="s1s", align_bytes=64)
+            for t2 in range(2):
+                src = s1raw[m][:, HALF * t2 : HALF * (t2 + 1)].rearrange(
+                    "p (g t r) -> p g r t", g=NC, t=4, r=64
+                )
+                nc.vector.tensor_copy(out=s1g[:, 0:4, t2], in_=src[:, 0:4])
+                nc.scalar.copy(out=s1g[:, 4:8, t2], in_=src[:, 4:8])
+            for hf in range(2):
+                sl = slice(4 * hf, 4 * hf + 4)
+                quant(
+                    cod[:, sl, :].rearrange("p c r -> p (c r)"),
+                    scl[:, sl, :].rearrange("p c r -> p (c r)"),
+                    s1g[:, sl].rearrange("p c a r t -> p (c a r t)"),
+                )
+            first_stage(("s1", m // 2), m % 2, cod, scl)
+            if m % 2 == 1:
+                h_copy(4, m // 2, ("s1", m // 2))
+        h_quant(4)
+        second_stage(4, False, True)
+
+        for q in range(4):
+            if q % 2 == 0:
+                nc.scalar.activation(
+                    out=osb[:, q, :], in_=acc[q][:, 0:NW], func=ACT.Identity,
+                    bias=b2[:, q : q + 1], scale=0.125,
+                )
+            else:
+                nc.vector.tensor_scalar(
+                    out=osb[:, q, :], in0=acc[q][:, 0:NW], scalar1=0.125,
+                    scalar2=b2[:, q : q + 1], op0=ALU.mult, op1=ALU.add,
+                )
+            nc.sync.dma_start(out=outv[:, q], in_=osb[:, q, :].rearrange("p (b s) -> p b s", b=4))

@@ -3,7 +3,7 @@ from contextlib import ExitStack
 import concourse.mybir as mybir
 from concourse.masks import make_identity
 
-PIN = True
+PIN = False
 
 FLOPS = 2 * 256 * 4096 * (512 + 2048) + 2 * 256 * 512 * (512 + 2048)
 

@@ -3,7 +3,7 @@ from contextlib import ExitStack
 import concourse.mybir as mybir
 from concourse.masks import make_identity
 
-PIN = False
+PIN = True
 
 FLOPS = 2 * 256 * 4096 * (512 + 2048) + 2 * 256 * 512 * (512 + 2048)
 
@@ -25,7 +25,7 @@ HALF = 2048
 def tile_skconv2d_pa_kernel(tc, xw, S1s, U1s, U2s, S2s, bias, out):
     nc = tc.nc
     u2v = U2s.rearrange("t r k -> (t r) k").rearrange("(g p j) k -> p g j k", p=P, j=4)
-    s1v = S1s.rearrange("t (a p e) r -> p t a (e r)", a=16, p=P, e=2)
+    s1v = S1s.rearrange("t (g p j) r -> p t g (j r)", g=NC, p=P, j=4)
     u1v = U1s.rearrange("t r o -> (t r) o").rearrange("(j p) o -> p j o", p=P)
     s2v = S2s.rearrange("t r o -> (t r) o").rearrange("(g p j) o -> p g j o", p=P, j=4)
     outv = out.rearrange("b (q p) i j -> p q b (i j)", p=P)
@@ -54,6 +54,8 @@ def tile_skconv2d_pa_kernel(tc, xw, S1s, U1s, U2s, S2s, bias, out):
 
         xq = const.tile([P, NC, NW], U32, name="xq", align_bytes=64)
         xs = const.tile([P, NC, NW], U8, name="xs", align_bytes=64)
+        yq = const.tile([P, NC, NW], U32, name="yq", align_bytes=64)
+        ys = const.tile([P, NC, NW], U8, name="ys", align_bytes=64)
         s2r = const.tile([P, 4, 4, 512], BF16, name="s2r")
         u1r = const.tile([P, 4, 512], BF16, name="u1r")
         wc = const.tile([P, 5, 512], U32, name="wc", align_bytes=64)
@@ -83,7 +85,7 @@ def tile_skconv2d_pa_kernel(tc, xw, S1s, U1s, U2s, S2s, bias, out):
                 t = rawp.tile([P, D], BF16, name="s1r", tag="raw")
                 for t2 in range(2):
                     nc.sync.dma_start(
-                        out=t[:, HALF * t2 : HALF * (t2 + 1)].rearrange("p (a x) -> p a x", a=16),
+                        out=t[:, HALF * t2 : HALF * (t2 + 1)].rearrange("p (a x) -> p a x", a=NC),
                         in_=s1v[:, 2 * m + t2],
                     )
                 s1raw[m] = t
@@ -99,36 +101,40 @@ def tile_skconv2d_pa_kernel(tc, xw, S1s, U1s, U2s, S2s, bias, out):
         def quant(codes, scales, src):
             nc.vector.quantize_mx(out=codes.bitcast(FP8X4), scales=scales, in_=src)
 
-        xg = []
+        def prepare_x(codes, scales, step):
+            xg = []
 
-        def quant_x(k):
-            quant(
-                xq[:, 2 * k : 2 * k + 2, :].rearrange("p c n -> p (c n)"),
-                xs[:, 2 * k : 2 * k + 2, :].rearrange("p c n -> p (c n)"),
-                xg[k // 2][:, 2 * (k % 2) : 2 * (k % 2) + 2].rearrange("p c n t -> p (c n t)"),
-            )
+            def quant_x(k):
+                quant(
+                    codes[:, 2 * k : 2 * k + 2, :].rearrange("p c n -> p (c n)"),
+                    scales[:, 2 * k : 2 * k + 2, :].rearrange("p c n -> p (c n)"),
+                    xg[k // 2][:, 2 * (k % 2) : 2 * (k % 2) + 2].rearrange("p c n t -> p (c n t)"),
+                )
 
-        for c in range(NC):
-            if c % 4 == 0:
-                xg.append(grpp.tile([P, 4, NW, 4], BF16, name="xg", tag="grp", align_bytes=64))
-            gf = xg[c // 4][:].bitcast(F32)
-            bank = tps.tile([P, 2, NW], F32, name="xb", tag="T")
-            for u in range(2):
-                for a in range(2):
-                    col = 256 * c + P * u
-                    nc.tensor.transpose(
-                        bank[:, u, P * a : P * (a + 1)],
-                        xr[a][:].bitcast(F32)[:, col : col + P],
-                        ident_f[:],
-                    )
-            src = bank[:].rearrange("p u n -> p n u")
-            if c % 2 == 0:
-                nc.vector.tensor_copy(out=gf[:, c % 4], in_=src)
-            else:
-                nc.scalar.copy(out=gf[:, c % 4], in_=src)
-            if c % 2 == 0 and c >= 2:
-                quant_x(c // 2 - 1)
-        quant_x(3)
+            for c in range(NC):
+                if c % 4 == 0:
+                    xg.append(grpp.tile([P, 4, NW, 4], BF16, name="xg", tag="grp", align_bytes=64))
+                gf = xg[c // 4][:].bitcast(F32)
+                bank = tps.tile([P, 2, NW], F32, name="xb", tag="T")
+                for u in range(2):
+                    for a in range(2):
+                        xf = xr[a][:].bitcast(F32)
+                        if step == 1:
+                            words = xf[:, 256 * c + P * u : 256 * c + P * (u + 1)]
+                        else:
+                            words = xf[:, 256 * c + u : 256 * (c + 1) : 2]
+                        nc.tensor.transpose(bank[:, u, P * a : P * (a + 1)], words, ident_f[:])
+                src = bank[:].rearrange("p u n -> p n u")
+                if c % 2 == 0:
+                    nc.vector.tensor_copy(out=gf[:, c % 4], in_=src)
+                else:
+                    nc.scalar.copy(out=gf[:, c % 4], in_=src)
+                if c % 2 == 0 and c >= 2:
+                    quant_x(c // 2 - 1)
+            quant_x(3)
+
+        prepare_x(xq, xs, 1)
+        prepare_x(yq, ys, 2)
         load_raw(6)
         load_raw(7)
 
@@ -171,7 +177,7 @@ def tile_skconv2d_pa_kernel(tc, xw, S1s, U1s, U2s, S2s, bias, out):
                     u2grp[i][:, sl].rearrange("p c r t -> p (c r t)"),
                 )
 
-        def first_stage(key, half, cod, scl):
+        def first_stage(key, half, cod, scl, xc, xsc):
             if half == 0:
                 hbank[key] = hps.tile([P, 2, NW], F32, name="hb", tag="h")
             hb = hbank[key]
@@ -180,8 +186,8 @@ def tile_skconv2d_pa_kernel(tc, xw, S1s, U1s, U2s, S2s, bias, out):
                     out=hb[:, half, :],
                     lhsT=cod[:, c, :].bitcast(FP8X4),
                     lhsT_scale=scl[:, c, :],
-                    rhs=xq[:, c, :].bitcast(FP8X4),
-                    rhs_scale=xs[:, c, :],
+                    rhs=xc[:, c, :].bitcast(FP8X4),
+                    rhs_scale=xsc[:, c, :],
                     start=(c == 0),
                     stop=(c == NC - 1),
                 )
@@ -219,7 +225,7 @@ def tile_skconv2d_pa_kernel(tc, xw, S1s, U1s, U2s, S2s, bias, out):
         quant_u2(1)
         for i in range(16):
             g, j = i // 4, i % 4
-            first_stage(("u2", i // 2), j % 2, u2cod[i][0], u2cod[i][1])
+            first_stage(("u2", i // 2), j % 2, u2cod[i][0], u2cod[i][1], xq, xs)
             if i + 2 < 16:
                 transposes(i + 2)
             if j % 2 == 1:
@@ -267,7 +273,7 @@ def tile_skconv2d_pa_kernel(tc, xw, S1s, U1s, U2s, S2s, bias, out):
                     scl[:, sl, :].rearrange("p c r -> p (c r)"),
                     s1g[:, sl].rearrange("p c a r t -> p (c a r t)"),
                 )
-            first_stage(("s1", m // 2), m % 2, cod, scl)
+            first_stage(("s1", m // 2), m % 2, cod, scl, yq, ys)
             if m % 2 == 1:
                 h_copy(4, m // 2, ("s1", m // 2))
         h_quant(4)

@@ -20,19 +20,34 @@ NW = 256
 D = 4096
 NC = 8
 HALF = 2048
+RAW_BUFS = 7
+S1_BUFS = 4
+S1_V = 6
+
+STREAM = (
+    ("u", 0), ("u", 1), ("u", 2), ("w", 4), ("u", 3), ("w", 0), ("w", 1), ("u", 4), ("w", 2),
+    ("u", 5), ("u", 6), ("u", 7), ("u", 8), ("w", 3), ("u", 9), ("u", 10), ("s", 0), ("s", 1),
+    ("u", 11), ("s", 2), ("u", 12), ("u", 13), ("s", 3), ("u", 14), ("s", 4), ("s", 5),
+    ("u", 15), ("s", 6), ("s", 7),
+)
+W_ROUND = {4: 1, 0: 2, 1: 3, 2: 4, 3: 8}
+S1_ROUND = (9, 9, 10, 12, 13, 13, 14, 14)
+PAIR_ROUND = (14, 15)
+S2_ROUND = 14
 
 
 def tile_skconv2d_pa_kernel(tc, xw, S1s, U1s, U2s, S2s, bias, out):
     nc = tc.nc
     u2v = U2s.rearrange("t r k -> (t r) k").rearrange("(g p j) k -> p g j k", p=P, j=4)
-    s1v = S1s.rearrange("t (g p j) r -> p t g (j r)", g=NC, p=P, j=4)
+    s1v = S1s.rearrange("t (a p e) r -> p t a (e r)", a=16, p=P, e=2)
     u1v = U1s.rearrange("t r o -> (t r) o").rearrange("(j p) o -> p j o", p=P)
     s2v = S2s.rearrange("t r o -> (t r) o").rearrange("(g p j) o -> p g j o", p=P, j=4)
     outv = out.rearrange("b (q p) i j -> p q b (i j)", p=P)
 
     with ExitStack() as ctx:
         const = ctx.enter_context(tc.tile_pool(name="const", bufs=1))
-        rawp = ctx.enter_context(tc.tile_pool(name="rawp", bufs=8))
+        rawp = ctx.enter_context(tc.tile_pool(name="rawp", bufs=RAW_BUFS))
+        s1rp = ctx.enter_context(tc.tile_pool(name="s1rp", bufs=S1_BUFS))
         grpp = ctx.enter_context(tc.tile_pool(name="grpp", bufs=3))
         codp = ctx.enter_context(tc.tile_pool(name="codp", bufs=3))
         s1gp = ctx.enter_context(tc.tile_pool(name="s1gp", bufs=2))
@@ -54,8 +69,6 @@ def tile_skconv2d_pa_kernel(tc, xw, S1s, U1s, U2s, S2s, bias, out):
 
         xq = const.tile([P, NC, NW], U32, name="xq", align_bytes=64)
         xs = const.tile([P, NC, NW], U8, name="xs", align_bytes=64)
-        yq = const.tile([P, NC, NW], U32, name="yq", align_bytes=64)
-        ys = const.tile([P, NC, NW], U8, name="ys", align_bytes=64)
         s2r = const.tile([P, 4, 4, 512], BF16, name="s2r")
         u1r = const.tile([P, 4, 512], BF16, name="u1r")
         wc = const.tile([P, 5, 512], U32, name="wc", align_bytes=64)
@@ -74,69 +87,69 @@ def tile_skconv2d_pa_kernel(tc, xw, S1s, U1s, U2s, S2s, bias, out):
                 )
         u2raw = {}
         s1raw = {}
+        state = {"ptr": 0, "u": RAW_BUFS - 2, "s": S1_BUFS}
 
-        def load_raw(n):
-            if n < 16:
-                t = rawp.tile([P, D], BF16, name="u2r", tag="raw")
-                nc.sync.dma_start(out=t[:], in_=u2v[:, n // 4, n % 4, :])
-                u2raw[n] = t
-            elif n < 20:
-                m = n - 16
-                t = rawp.tile([P, D], BF16, name="s1r", tag="raw")
-                for t2 in range(2):
-                    nc.sync.dma_start(
-                        out=t[:, HALF * t2 : HALF * (t2 + 1)].rearrange("p (a x) -> p a x", a=NC),
-                        in_=s1v[:, 2 * m + t2],
-                    )
-                s1raw[m] = t
-            if n == 3:
-                nc.sync.dma_start(out=u1r[:], in_=u1v)
-            if n in (5, 7, 9, 11):
-                g = (n - 5) // 2
-                nc.sync.dma_start(out=s2r[:, g], in_=s2v[:, g])
+        def pump():
+            while state["ptr"] < len(STREAM):
+                kind, n = STREAM[state["ptr"]]
+                if kind != "w" and state[kind] == 0:
+                    break
+                if kind == "u":
+                    t = rawp.tile([P, D], BF16, name="u2r", tag="raw")
+                    nc.sync.dma_start(out=t[:], in_=u2v[:, n // 4, n % 4, :])
+                    u2raw[n] = t
+                    state["u"] = state["u"] - 1
+                elif kind == "s":
+                    t = s1rp.tile([P, HALF], BF16, name="s1r", tag="s1r")
+                    nc.sync.dma_start(out=t[:].rearrange("p (a x) -> p a x", a=16), in_=s1v[:, n])
+                    s1raw[n] = t
+                    state["s"] = state["s"] - 1
+                elif n == 4:
+                    nc.sync.dma_start(out=u1r[:], in_=u1v)
+                else:
+                    nc.sync.dma_start(out=s2r[:, n], in_=s2v[:, n])
+                state["ptr"] = state["ptr"] + 1
 
-        for n in range(6):
-            load_raw(n)
+        def freed(kind, count):
+            state[kind] = state[kind] + count
+            pump()
+
+        pump()
 
         def quant(codes, scales, src):
             nc.vector.quantize_mx(out=codes.bitcast(FP8X4), scales=scales, in_=src)
 
-        def prepare_x(codes, scales, step):
-            xg = []
+        xg = []
 
-            def quant_x(k):
-                quant(
-                    codes[:, 2 * k : 2 * k + 2, :].rearrange("p c n -> p (c n)"),
-                    scales[:, 2 * k : 2 * k + 2, :].rearrange("p c n -> p (c n)"),
-                    xg[k // 2][:, 2 * (k % 2) : 2 * (k % 2) + 2].rearrange("p c n t -> p (c n t)"),
-                )
+        def quant_x(k):
+            quant(
+                xq[:, 2 * k : 2 * k + 2, :].rearrange("p c n -> p (c n)"),
+                xs[:, 2 * k : 2 * k + 2, :].rearrange("p c n -> p (c n)"),
+                xg[k // 2][:, 2 * (k % 2) : 2 * (k % 2) + 2].rearrange("p c n t -> p (c n t)"),
+            )
 
-            for c in range(NC):
-                if c % 4 == 0:
-                    xg.append(grpp.tile([P, 4, NW, 4], BF16, name="xg", tag="grp", align_bytes=64))
-                gf = xg[c // 4][:].bitcast(F32)
-                bank = tps.tile([P, 2, NW], F32, name="xb", tag="T")
-                for u in range(2):
-                    for a in range(2):
-                        xf = xr[a][:].bitcast(F32)
-                        if step == 1:
-                            words = xf[:, 256 * c + P * u : 256 * c + P * (u + 1)]
-                        else:
-                            words = xf[:, 256 * c + u : 256 * (c + 1) : 2]
-                        nc.tensor.transpose(bank[:, u, P * a : P * (a + 1)], words, ident_f[:])
-                src = bank[:].rearrange("p u n -> p n u")
-                if c % 2 == 0:
-                    nc.vector.tensor_copy(out=gf[:, c % 4], in_=src)
-                else:
-                    nc.scalar.copy(out=gf[:, c % 4], in_=src)
-                if c % 2 == 0 and c >= 2:
-                    quant_x(c // 2 - 1)
-            quant_x(3)
-
-        prepare_x(xq, xs, 1)
-        prepare_x(yq, ys, 2)
-        load_raw(6)
-        load_raw(7)
+        for c in range(NC):
+            if c % 4 == 0:
+                xg.append(grpp.tile([P, 4, NW, 4], BF16, name="xg", tag="grp", align_bytes=64))
+            gf = xg[c // 4][:].bitcast(F32)
+            bank = tps.tile([P, 2, NW], F32, name="xb", tag="T")
+            for u in range(2):
+                for a in range(2):
+                    col = 256 * c + P * u
+                    nc.tensor.transpose(
+                        bank[:, u, P * a : P * (a + 1)],
+                        xr[a][:].bitcast(F32)[:, col : col + P],
+                        ident_f[:],
+                    )
+            src = bank[:].rearrange("p u n -> p n u")
+            if c % 2 == 0:
+                nc.vector.tensor_copy(out=gf[:, c % 4], in_=src)
+            else:
+                nc.scalar.copy(out=gf[:, c % 4], in_=src)
+            if c % 2 == 0 and c >= 2:
+                quant_x(c // 2 - 1)
+        quant_x(3)
+        freed("u", 2)
 
         bt = tps.tile([P, P], BF16, name="bt", tag="T")
         nc.tensor.transpose(bt[:], bz[:], ident_b[:])
@@ -159,11 +172,11 @@ def tile_skconv2d_pa_kernel(tc, xw, S1s, U1s, U2s, S2s, bias, out):
                         col = 256 * (2 * b + c2) + P * u
                         nc.tensor.transpose(bank[:, c2, u, :], rf[:, col : col + P], ident_f[:])
                 src = bank[:].rearrange("p c u r -> p c r u")
-                if b == 0 and i % 2 == 1:
+                if (b == 0 and i % 2 == 1) or (i >= 14 and b % 2 == 0):
                     nc.vector.tensor_copy(out=gf[:, 2 * b : 2 * b + 2], in_=src)
                 else:
                     nc.scalar.copy(out=gf[:, 2 * b : 2 * b + 2], in_=src)
-            load_raw(8 + i)
+            freed("u", 1)
 
         def quant_u2(i):
             cod = codp.tile([P, NC, P], U32, name="u2c", tag="u2c", align_bytes=64)
@@ -177,17 +190,19 @@ def tile_skconv2d_pa_kernel(tc, xw, S1s, U1s, U2s, S2s, bias, out):
                     u2grp[i][:, sl].rearrange("p c r t -> p (c r t)"),
                 )
 
-        def first_stage(key, half, cod, scl, xc, xsc):
-            if half == 0:
+        def first_stage(key, half, cod, scl):
+            if half == 0 and key[0] == "u2":
                 hbank[key] = hps.tile([P, 2, NW], F32, name="hb", tag="h")
+            elif half == 0:
+                hbank[key] = tps.tile([P, 2, NW], F32, name="hb1", tag="T")
             hb = hbank[key]
             for c in range(NC):
                 nc.tensor.matmul_mx(
                     out=hb[:, half, :],
                     lhsT=cod[:, c, :].bitcast(FP8X4),
                     lhsT_scale=scl[:, c, :],
-                    rhs=xc[:, c, :].bitcast(FP8X4),
-                    rhs_scale=xsc[:, c, :],
+                    rhs=xq[:, c, :].bitcast(FP8X4),
+                    rhs_scale=xs[:, c, :],
                     start=(c == 0),
                     stop=(c == NC - 1),
                 )
@@ -217,31 +232,12 @@ def tile_skconv2d_pa_kernel(tc, xw, S1s, U1s, U2s, S2s, bias, out):
         def w_quant(s):
             quant(wc[:, s, :], ws[:, s, :], wgrp[s][:].rearrange("p o t -> p (o t)"))
 
-        w_order = {4: 4, 6: 0, 8: 1, 10: 2, 12: 3}
-
-        transposes(0)
-        quant_u2(0)
-        transposes(1)
-        quant_u2(1)
-        for i in range(16):
-            g, j = i // 4, i % 4
-            first_stage(("u2", i // 2), j % 2, u2cod[i][0], u2cod[i][1], xq, xs)
-            if i + 2 < 16:
-                transposes(i + 2)
-            if j % 2 == 1:
-                h_copy(g, j // 2, ("u2", i // 2))
-            if i + 2 < 16:
-                quant_u2(i + 2)
-            if j == 3:
-                h_quant(g)
-            if i in w_order:
-                w_regroup(w_order[i])
-            if i - 1 in w_order:
-                w_quant(w_order[i - 1])
-
-        acc = [tps.tile([P, 512], F32, name="acc%d" % q, tag="T") for q in range(4)]
+        acc = []
 
         def second_stage(s, start, stop):
+            if start:
+                for q in range(4):
+                    acc.append(tps.tile([P, 512], F32, name="acc%d" % q, tag="T"))
             for q in range(4):
                 nc.tensor.matmul_mx(
                     out=acc[q][:, 0:NW],
@@ -253,29 +249,65 @@ def tile_skconv2d_pa_kernel(tc, xw, S1s, U1s, U2s, S2s, bias, out):
                     stop=stop,
                 )
 
-        for g in range(4):
-            second_stage(g, g == 0, False)
+        s1grp = {}
+        s1cod = {}
 
-        for m in range(4):
-            s1g = s1gp.tile([P, NC, 2, 64, 4], BF16, name="s1g", tag="s1g", align_bytes=64)
+        def s1_regroup(t):
+            m, t2 = t // 2, t % 2
+            if t2 == 0:
+                s1grp[m] = s1gp.tile([P, NC, 2, 64, 4], BF16, name="s1g", tag="s1g", align_bytes=64)
+            src = s1raw[t][:].rearrange("p (g t r) -> p g r t", g=NC, t=4, r=64)
+            nc.vector.tensor_copy(out=s1grp[m][:, 0:S1_V, t2], in_=src[:, 0:S1_V])
+            nc.scalar.copy(out=s1grp[m][:, S1_V:NC, t2], in_=src[:, S1_V:NC])
+            freed("s", 1)
+
+        def s1_quant(m):
             cod = s1cp.tile([P, NC, P], U32, name="s1c", tag="s1c", align_bytes=64)
             scl = s1cp.tile([P, NC, P], U8, name="s1s", tag="s1s", align_bytes=64)
-            for t2 in range(2):
-                src = s1raw[m][:, HALF * t2 : HALF * (t2 + 1)].rearrange(
-                    "p (g t r) -> p g r t", g=NC, t=4, r=64
-                )
-                nc.vector.tensor_copy(out=s1g[:, 0:4, t2], in_=src[:, 0:4])
-                nc.scalar.copy(out=s1g[:, 4:8, t2], in_=src[:, 4:8])
+            s1cod[m] = (cod, scl)
             for hf in range(2):
                 sl = slice(4 * hf, 4 * hf + 4)
                 quant(
                     cod[:, sl, :].rearrange("p c r -> p (c r)"),
                     scl[:, sl, :].rearrange("p c r -> p (c r)"),
-                    s1g[:, sl].rearrange("p c a r t -> p (c a r t)"),
+                    s1grp[m][:, sl].rearrange("p c a r t -> p (c a r t)"),
                 )
-            first_stage(("s1", m // 2), m % 2, cod, scl, yq, ys)
-            if m % 2 == 1:
-                h_copy(4, m // 2, ("s1", m // 2))
+
+        transposes(0)
+        quant_u2(0)
+        transposes(1)
+        quant_u2(1)
+        for i in range(16):
+            g, j = i // 4, i % 4
+            first_stage(("u2", i // 2), j % 2, u2cod[i][0], u2cod[i][1])
+            if j % 2 == 1:
+                h_copy(g, j // 2, ("u2", i // 2))
+            for pr in range(2):
+                if PAIR_ROUND[pr] == i:
+                    for m in (2 * pr, 2 * pr + 1):
+                        first_stage(("s1", pr), m % 2, s1cod[m][0], s1cod[m][1])
+                    h_copy(4, pr, ("s1", pr))
+            if i + 2 < 16:
+                transposes(i + 2)
+            if i == S2_ROUND:
+                for s in range(3):
+                    second_stage(s, s == 0, False)
+            for t in range(8):
+                if S1_ROUND[t] == i:
+                    s1_regroup(t)
+                    if t % 2 == 1:
+                        s1_quant(t // 2)
+            for s in (4, 0, 1, 2, 3):
+                if W_ROUND[s] + 1 == i:
+                    w_quant(s)
+                if W_ROUND[s] == i:
+                    w_regroup(s)
+            if j == 0 and i > 0:
+                h_quant(g - 1)
+            if i + 2 < 16:
+                quant_u2(i + 2)
+        h_quant(3)
+        second_stage(3, False, False)
         h_quant(4)
         second_stage(4, False, True)
 

@@ -26,7 +26,7 @@ S1_V = 6
 
 STREAM = (
     ("u", 0), ("u", 1), ("u", 2), ("w", 4), ("u", 3), ("w", 0), ("w", 1), ("u", 4), ("w", 2),
-    ("u", 5), ("u", 6), ("u", 7), ("u", 8), ("w", 3), ("u", 9), ("u", 10), ("s", 0), ("s", 1),
+    ("u", 5), ("u", 6), ("d", 0), ("u", 7), ("u", 8), ("d", 0), ("w", 3), ("u", 9), ("u", 10), ("d", 0), ("s", 0), ("s", 1),
     ("u", 11), ("s", 2), ("u", 12), ("u", 13), ("s", 3), ("u", 14), ("s", 4), ("s", 5),
     ("u", 15), ("s", 6), ("s", 7),
 )
@@ -77,6 +77,7 @@ def tile_skconv2d_pa_kernel(tc, xw, S1s, U1s, U2s, S2s, bias, out):
         hqs = const.tile([P, 5, NW], U8, name="hqs", align_bytes=64)
         osb = const.tile([P, 4, NW], F32, name="osb")
         b2 = const.tile([P, 4], F32, name="b2")
+        dummy = const.tile([P, D], BF16, name="dummy")
 
         xr = [rawp.tile([P, D], BF16, name="xr%d" % a, tag="raw") for a in range(2)]
         for hf in range(2):
@@ -92,7 +93,7 @@ def tile_skconv2d_pa_kernel(tc, xw, S1s, U1s, U2s, S2s, bias, out):
         def pump():
             while state["ptr"] < len(STREAM):
                 kind, n = STREAM[state["ptr"]]
-                if kind != "w" and state[kind] == 0:
+                if kind in ("u", "s") and state[kind] == 0:
                     break
                 if kind == "u":
                     t = rawp.tile([P, D], BF16, name="u2r", tag="raw")
@@ -104,6 +105,8 @@ def tile_skconv2d_pa_kernel(tc, xw, S1s, U1s, U2s, S2s, bias, out):
                     nc.sync.dma_start(out=t[:].rearrange("p (a x) -> p a x", a=16), in_=s1v[:, n])
                     s1raw[n] = t
                     state["s"] = state["s"] - 1
+                elif kind == "d":
+                    nc.sync.dma_start(out=dummy[:], in_=u2v[:, 0, 0, :])
                 elif n == 4:
                     nc.sync.dma_start(out=u1r[:], in_=u1v)
                 else:
@@ -171,6 +174,9 @@ def tile_skconv2d_pa_kernel(tc, xw, S1s, U1s, U2s, S2s, bias, out):
                     for u in range(2):
                         col = 256 * (2 * b + c2) + P * u
                         nc.tensor.transpose(bank[:, c2, u, :], rf[:, col : col + P], ident_f[:])
+                if b == 3 and 4 <= i < 12:
+                    for rep in range(2):
+                        nc.tensor.transpose(bank[:, 1, 1, :], rf[:, 1920:2048], ident_f[:])
                 src = bank[:].rearrange("p c u r -> p c r u")
                 if (b == 0 and i % 2 == 1) or (i >= 14 and b % 2 == 0):
                     nc.vector.tensor_copy(out=gf[:, 2 * b : 2 * b + 2], in_=src)
@@ -182,7 +188,7 @@ def tile_skconv2d_pa_kernel(tc, xw, S1s, U1s, U2s, S2s, bias, out):
             cod = codp.tile([P, NC, P], U32, name="u2c", tag="u2c", align_bytes=64)
             scl = codp.tile([P, NC, P], U8, name="u2s", tag="u2s", align_bytes=64)
             u2cod[i] = (cod, scl)
-            for hf in range(2):
+            for hf in (0, 1, 1) if 4 <= i < 10 else (0, 1):
                 sl = slice(4 * hf, 4 * hf + 4)
                 quant(
                     cod[:, sl, :].rearrange("p c r -> p (c r)"),

@@ -25,21 +25,20 @@ S1_BUFS = 4
 S1_V = 6
 
 STREAM = (
-    ("u", 0), ("u", 1), ("u", 2), ("w", 4), ("u", 3), ("w", 0), ("w", 1), ("u", 4), ("w", 2),
-    ("u", 5), ("u", 6), ("d", 0), ("u", 7), ("u", 8), ("d", 0), ("w", 3), ("u", 9), ("u", 10), ("d", 0), ("s", 0), ("s", 1),
-    ("u", 11), ("s", 2), ("u", 12), ("u", 13), ("s", 3), ("u", 14), ("s", 4), ("s", 5),
-    ("u", 15), ("s", 6), ("s", 7),
+    ("u", 0), ("u", 1), ("s", 0), ("u", 2), ("s", 1), ("u", 3), ("s", 2), ("u", 4), ("w", 4),
+    ("u", 5), ("w", 0), ("u", 6), ("u", 7), ("s", 3), ("s", 4), ("u", 8), ("u", 9), ("s", 5),
+    ("u", 10), ("w", 1), ("u", 11), ("s", 6), ("u", 12), ("s", 7), ("w", 2), ("u", 13), ("w", 3),
+    ("u", 14), ("u", 15),
 )
-W_ROUND = {4: 1, 0: 2, 1: 3, 2: 4, 3: 8}
-S1_ROUND = (9, 9, 10, 12, 13, 13, 14, 14)
-PAIR_ROUND = (14, 15)
-S2_ROUND = 14
-
+W_ROUND = {4: 3, 0: 5, 1: 10, 2: 11, 3: 14}
+S1_ROUND = (0, 1, 3, 6, 7, 8, 10, 11)
+Q1_ROUND = (2, 7, 9, 12)
+PAIR_ROUND = (9, 13)
 
 def tile_skconv2d_pa_kernel(tc, xw, S1s, U1s, U2s, S2s, bias, out):
     nc = tc.nc
     u2v = U2s.rearrange("t r k -> (t r) k").rearrange("(g p j) k -> p g j k", p=P, j=4)
-    s1v = S1s.rearrange("t (a p e) r -> p t a (e r)", a=16, p=P, e=2)
+    s1v = S1s.rearrange("t (g p j) r -> p t g (j r)", g=NC, p=P, j=4)
     u1v = U1s.rearrange("t r o -> (t r) o").rearrange("(j p) o -> p j o", p=P)
     s2v = S2s.rearrange("t r o -> (t r) o").rearrange("(g p j) o -> p g j o", p=P, j=4)
     outv = out.rearrange("b (q p) i j -> p q b (i j)", p=P)
@@ -69,6 +68,8 @@ def tile_skconv2d_pa_kernel(tc, xw, S1s, U1s, U2s, S2s, bias, out):
 
         xq = const.tile([P, NC, NW], U32, name="xq", align_bytes=64)
         xs = const.tile([P, NC, NW], U8, name="xs", align_bytes=64)
+        yq = const.tile([P, NC, NW], U32, name="yq", align_bytes=64)
+        ys = const.tile([P, NC, NW], U8, name="ys", align_bytes=64)
         s2r = const.tile([P, 4, 4, 512], BF16, name="s2r")
         u1r = const.tile([P, 4, 512], BF16, name="u1r")
         wc = const.tile([P, 5, 512], U32, name="wc", align_bytes=64)
@@ -77,7 +78,6 @@ def tile_skconv2d_pa_kernel(tc, xw, S1s, U1s, U2s, S2s, bias, out):
         hqs = const.tile([P, 5, NW], U8, name="hqs", align_bytes=64)
         osb = const.tile([P, 4, NW], F32, name="osb")
         b2 = const.tile([P, 4], F32, name="b2")
-        dummy = const.tile([P, D], BF16, name="dummy")
 
         xr = [rawp.tile([P, D], BF16, name="xr%d" % a, tag="raw") for a in range(2)]
         for hf in range(2):
@@ -93,7 +93,7 @@ def tile_skconv2d_pa_kernel(tc, xw, S1s, U1s, U2s, S2s, bias, out):
         def pump():
             while state["ptr"] < len(STREAM):
                 kind, n = STREAM[state["ptr"]]
-                if kind in ("u", "s") and state[kind] == 0:
+                if kind != "w" and state[kind] == 0:
                     break
                 if kind == "u":
                     t = rawp.tile([P, D], BF16, name="u2r", tag="raw")
@@ -102,13 +102,13 @@ def tile_skconv2d_pa_kernel(tc, xw, S1s, U1s, U2s, S2s, bias, out):
                     state["u"] = state["u"] - 1
                 elif kind == "s":
                     t = s1rp.tile([P, HALF], BF16, name="s1r", tag="s1r")
-                    nc.sync.dma_start(out=t[:].rearrange("p (a x) -> p a x", a=16), in_=s1v[:, n])
+                    for g in range(NC):
+                        nc.sync.dma_start(out=t[:, 256 * g : 256 * (g + 1)], in_=s1v[:, n, g])
                     s1raw[n] = t
                     state["s"] = state["s"] - 1
-                elif kind == "d":
-                    nc.sync.dma_start(out=dummy[:], in_=u2v[:, 0, 0, :])
                 elif n == 4:
-                    nc.sync.dma_start(out=u1r[:], in_=u1v)
+                    for j in range(4):
+                        nc.sync.dma_start(out=u1r[:, j], in_=u1v[:, j])
                 else:
                     nc.sync.dma_start(out=s2r[:, n], in_=s2v[:, n])
                 state["ptr"] = state["ptr"] + 1
@@ -122,36 +122,40 @@ def tile_skconv2d_pa_kernel(tc, xw, S1s, U1s, U2s, S2s, bias, out):
         def quant(codes, scales, src):
             nc.vector.quantize_mx(out=codes.bitcast(FP8X4), scales=scales, in_=src)
 
-        xg = []
+        def prepare_x(codes, scales, step):
+            xg = []
 
-        def quant_x(k):
-            quant(
-                xq[:, 2 * k : 2 * k + 2, :].rearrange("p c n -> p (c n)"),
-                xs[:, 2 * k : 2 * k + 2, :].rearrange("p c n -> p (c n)"),
-                xg[k // 2][:, 2 * (k % 2) : 2 * (k % 2) + 2].rearrange("p c n t -> p (c n t)"),
-            )
+            def quant_x(k):
+                quant(
+                    codes[:, 2 * k : 2 * k + 2, :].rearrange("p c n -> p (c n)"),
+                    scales[:, 2 * k : 2 * k + 2, :].rearrange("p c n -> p (c n)"),
+                    xg[k // 2][:, 2 * (k % 2) : 2 * (k % 2) + 2].rearrange("p c n t -> p (c n t)"),
+                )
 
-        for c in range(NC):
-            if c % 4 == 0:
-                xg.append(grpp.tile([P, 4, NW, 4], BF16, name="xg", tag="grp", align_bytes=64))
-            gf = xg[c // 4][:].bitcast(F32)
-            bank = tps.tile([P, 2, NW], F32, name="xb", tag="T")
-            for u in range(2):
-                for a in range(2):
-                    col = 256 * c + P * u
-                    nc.tensor.transpose(
-                        bank[:, u, P * a : P * (a + 1)],
-                        xr[a][:].bitcast(F32)[:, col : col + P],
-                        ident_f[:],
-                    )
-            src = bank[:].rearrange("p u n -> p n u")
-            if c % 2 == 0:
-                nc.vector.tensor_copy(out=gf[:, c % 4], in_=src)
-            else:
-                nc.scalar.copy(out=gf[:, c % 4], in_=src)
-            if c % 2 == 0 and c >= 2:
-                quant_x(c // 2 - 1)
-        quant_x(3)
+            for c in range(NC):
+                if c % 4 == 0:
+                    xg.append(grpp.tile([P, 4, NW, 4], BF16, name="xg", tag="grp", align_bytes=64))
+                gf = xg[c // 4][:].bitcast(F32)
+                bank = tps.tile([P, 2, NW], F32, name="xb", tag="T")
+                for u in range(2):
+                    for a in range(2):
+                        xf = xr[a][:].bitcast(F32)
+                        if step == 1:
+                            words = xf[:, 256 * c + P * u : 256 * c + P * (u + 1)]
+                        else:
+                            words = xf[:, 256 * c + u : 256 * (c + 1) : 2]
+                        nc.tensor.transpose(bank[:, u, P * a : P * (a + 1)], words, ident_f[:])
+                src = bank[:].rearrange("p u n -> p n u")
+                if c % 2 == 0:
+                    nc.vector.tensor_copy(out=gf[:, c % 4], in_=src)
+                else:
+                    nc.scalar.copy(out=gf[:, c % 4], in_=src)
+                if c % 2 == 0 and c >= 2:
+                    quant_x(c // 2 - 1)
+            quant_x(3)
+
+        prepare_x(xq, xs, 1)
+        prepare_x(yq, ys, 2)
         freed("u", 2)
 
         bt = tps.tile([P, P], BF16, name="bt", tag="T")
@@ -174,11 +178,8 @@ def tile_skconv2d_pa_kernel(tc, xw, S1s, U1s, U2s, S2s, bias, out):
                     for u in range(2):
                         col = 256 * (2 * b + c2) + P * u
                         nc.tensor.transpose(bank[:, c2, u, :], rf[:, col : col + P], ident_f[:])
-                if b == 3 and 4 <= i < 12:
-                    for rep in range(2):
-                        nc.tensor.transpose(bank[:, 1, 1, :], rf[:, 1920:2048], ident_f[:])
                 src = bank[:].rearrange("p c u r -> p c r u")
-                if (b == 0 and i % 2 == 1) or (i >= 14 and b % 2 == 0):
+                if i >= 14 and b % 2 == 0:
                     nc.vector.tensor_copy(out=gf[:, 2 * b : 2 * b + 2], in_=src)
                 else:
                     nc.scalar.copy(out=gf[:, 2 * b : 2 * b + 2], in_=src)
@@ -188,7 +189,7 @@ def tile_skconv2d_pa_kernel(tc, xw, S1s, U1s, U2s, S2s, bias, out):
             cod = codp.tile([P, NC, P], U32, name="u2c", tag="u2c", align_bytes=64)
             scl = codp.tile([P, NC, P], U8, name="u2s", tag="u2s", align_bytes=64)
             u2cod[i] = (cod, scl)
-            for hf in (0, 1, 1) if 4 <= i < 10 else (0, 1):
+            for hf in range(2):
                 sl = slice(4 * hf, 4 * hf + 4)
                 quant(
                     cod[:, sl, :].rearrange("p c r -> p (c r)"),
@@ -196,7 +197,7 @@ def tile_skconv2d_pa_kernel(tc, xw, S1s, U1s, U2s, S2s, bias, out):
                     u2grp[i][:, sl].rearrange("p c r t -> p (c r t)"),
                 )
 
-        def first_stage(key, half, cod, scl):
+        def first_stage(key, half, cod, scl, xc, xsc):
             if half == 0 and key[0] == "u2":
                 hbank[key] = hps.tile([P, 2, NW], F32, name="hb", tag="h")
             elif half == 0:
@@ -207,8 +208,8 @@ def tile_skconv2d_pa_kernel(tc, xw, S1s, U1s, U2s, S2s, bias, out):
                     out=hb[:, half, :],
                     lhsT=cod[:, c, :].bitcast(FP8X4),
                     lhsT_scale=scl[:, c, :],
-                    rhs=xq[:, c, :].bitcast(FP8X4),
-                    rhs_scale=xs[:, c, :],
+                    rhs=xc[:, c, :].bitcast(FP8X4),
+                    rhs_scale=xsc[:, c, :],
                     start=(c == 0),
                     stop=(c == NC - 1),
                 )
@@ -285,24 +286,25 @@ def tile_skconv2d_pa_kernel(tc, xw, S1s, U1s, U2s, S2s, bias, out):
         quant_u2(1)
         for i in range(16):
             g, j = i // 4, i % 4
-            first_stage(("u2", i // 2), j % 2, u2cod[i][0], u2cod[i][1])
+            first_stage(("u2", i // 2), j % 2, u2cod[i][0], u2cod[i][1], xq, xs)
             if j % 2 == 1:
                 h_copy(g, j // 2, ("u2", i // 2))
             for pr in range(2):
                 if PAIR_ROUND[pr] == i:
                     for m in (2 * pr, 2 * pr + 1):
-                        first_stage(("s1", pr), m % 2, s1cod[m][0], s1cod[m][1])
+                        first_stage(("s1", pr), m % 2, s1cod[m][0], s1cod[m][1], yq, ys)
                     h_copy(4, pr, ("s1", pr))
             if i + 2 < 16:
                 transposes(i + 2)
-            if i == S2_ROUND:
-                for s in range(3):
+            if i == 15:
+                for s in (0, 1, 2, 4):
                     second_stage(s, s == 0, False)
             for t in range(8):
                 if S1_ROUND[t] == i:
                     s1_regroup(t)
-                    if t % 2 == 1:
-                        s1_quant(t // 2)
+            for m in range(4):
+                if Q1_ROUND[m] == i:
+                    s1_quant(m)
             for s in (4, 0, 1, 2, 3):
                 if W_ROUND[s] + 1 == i:
                     w_quant(s)
@@ -310,12 +312,12 @@ def tile_skconv2d_pa_kernel(tc, xw, S1s, U1s, U2s, S2s, bias, out):
                     w_regroup(s)
             if j == 0 and i > 0:
                 h_quant(g - 1)
+            if i == PAIR_ROUND[1] + 1:
+                h_quant(4)
             if i + 2 < 16:
                 quant_u2(i + 2)
         h_quant(3)
-        second_stage(3, False, False)
-        h_quant(4)
-        second_stage(4, False, True)
+        second_stage(3, False, True)
 
         for q in range(4):
             if q % 2 == 0:

@@ -25,20 +25,21 @@ S1_BUFS = 4
 S1_V = 6
 
 STREAM = (
-    ("u", 0), ("u", 1), ("s", 0), ("u", 2), ("s", 1), ("u", 3), ("s", 2), ("u", 4), ("w", 4),
-    ("u", 5), ("w", 0), ("u", 6), ("u", 7), ("s", 3), ("s", 4), ("u", 8), ("u", 9), ("s", 5),
-    ("u", 10), ("w", 1), ("u", 11), ("s", 6), ("u", 12), ("s", 7), ("w", 2), ("u", 13), ("w", 3),
-    ("u", 14), ("u", 15),
+    ("u", 0), ("u", 1), ("u", 2), ("w", 4), ("u", 3), ("w", 0), ("w", 1), ("u", 4), ("w", 2),
+    ("u", 5), ("u", 6), ("u", 7), ("u", 8), ("w", 3), ("u", 9), ("u", 10), ("s", 0), ("s", 1),
+    ("u", 11), ("s", 2), ("u", 12), ("u", 13), ("s", 3), ("u", 14), ("s", 4), ("s", 5),
+    ("u", 15), ("s", 6), ("s", 7),
 )
-W_ROUND = {4: 3, 0: 5, 1: 10, 2: 11, 3: 14}
-S1_ROUND = (0, 1, 3, 6, 7, 8, 10, 11)
-Q1_ROUND = (2, 7, 9, 12)
-PAIR_ROUND = (9, 13)
+W_ROUND = {4: 1, 0: 2, 1: 3, 2: 4, 3: 8}
+S1_ROUND = (9, 9, 10, 12, 13, 13, 14, 14)
+PAIR_ROUND = (14, 15)
+S2_ROUND = 14
+
 
 def tile_skconv2d_pa_kernel(tc, xw, S1s, U1s, U2s, S2s, bias, out):
     nc = tc.nc
     u2v = U2s.rearrange("t r k -> (t r) k").rearrange("(g p j) k -> p g j k", p=P, j=4)
-    s1v = S1s.rearrange("t (g p j) r -> p t g (j r)", g=NC, p=P, j=4)
+    s1v = S1s.rearrange("t (a p e) r -> p t a (e r)", a=16, p=P, e=2)
     u1v = U1s.rearrange("t r o -> (t r) o").rearrange("(j p) o -> p j o", p=P)
     s2v = S2s.rearrange("t r o -> (t r) o").rearrange("(g p j) o -> p g j o", p=P, j=4)
     outv = out.rearrange("b (q p) i j -> p q b (i j)", p=P)
@@ -68,8 +69,6 @@ def tile_skconv2d_pa_kernel(tc, xw, S1s, U1s, U2s, S2s, bias, out):
 
         xq = const.tile([P, NC, NW], U32, name="xq", align_bytes=64)
         xs = const.tile([P, NC, NW], U8, name="xs", align_bytes=64)
-        yq = const.tile([P, NC, NW], U32, name="yq", align_bytes=64)
-        ys = const.tile([P, NC, NW], U8, name="ys", align_bytes=64)
         s2r = const.tile([P, 4, 4, 512], BF16, name="s2r")
         u1r = const.tile([P, 4, 512], BF16, name="u1r")
         wc = const.tile([P, 5, 512], U32, name="wc", align_bytes=64)
@@ -102,13 +101,15 @@ def tile_skconv2d_pa_kernel(tc, xw, S1s, U1s, U2s, S2s, bias, out):
                     state["u"] = state["u"] - 1
                 elif kind == "s":
                     t = s1rp.tile([P, HALF], BF16, name="s1r", tag="s1r")
-                    for g in range(NC):
-                        nc.sync.dma_start(out=t[:, 256 * g : 256 * (g + 1)], in_=s1v[:, n, g])
+                    for q in range(4):
+                        nc.sync.dma_start(
+                            out=t[:, 512 * q : 512 * (q + 1)].rearrange("p (a x) -> p a x", a=4),
+                            in_=s1v[:, n, 4 * q : 4 * (q + 1)],
+                        )
                     s1raw[n] = t
                     state["s"] = state["s"] - 1
                 elif n == 4:
-                    for j in range(4):
-                        nc.sync.dma_start(out=u1r[:, j], in_=u1v[:, j])
+                    nc.sync.dma_start(out=u1r[:], in_=u1v)
                 else:
                     nc.sync.dma_start(out=s2r[:, n], in_=s2v[:, n])
                 state["ptr"] = state["ptr"] + 1
@@ -122,40 +123,36 @@ def tile_skconv2d_pa_kernel(tc, xw, S1s, U1s, U2s, S2s, bias, out):
         def quant(codes, scales, src):
             nc.vector.quantize_mx(out=codes.bitcast(FP8X4), scales=scales, in_=src)
 
-        def prepare_x(codes, scales, step):
-            xg = []
+        xg = []
 
-            def quant_x(k):
-                quant(
-                    codes[:, 2 * k : 2 * k + 2, :].rearrange("p c n -> p (c n)"),
-                    scales[:, 2 * k : 2 * k + 2, :].rearrange("p c n -> p (c n)"),
-                    xg[k // 2][:, 2 * (k % 2) : 2 * (k % 2) + 2].rearrange("p c n t -> p (c n t)"),
-                )
+        def quant_x(k):
+            quant(
+                xq[:, 2 * k : 2 * k + 2, :].rearrange("p c n -> p (c n)"),
+                xs[:, 2 * k : 2 * k + 2, :].rearrange("p c n -> p (c n)"),
+                xg[k // 2][:, 2 * (k % 2) : 2 * (k % 2) + 2].rearrange("p c n t -> p (c n t)"),
+            )
 
-            for c in range(NC):
-                if c % 4 == 0:
-                    xg.append(grpp.tile([P, 4, NW, 4], BF16, name="xg", tag="grp", align_bytes=64))
-                gf = xg[c // 4][:].bitcast(F32)
-                bank = tps.tile([P, 2, NW], F32, name="xb", tag="T")
-                for u in range(2):
-                    for a in range(2):
-                        xf = xr[a][:].bitcast(F32)
-                        if step == 1:
-                            words = xf[:, 256 * c + P * u : 256 * c + P * (u + 1)]
-                        else:
-                            words = xf[:, 256 * c + u : 256 * (c + 1) : 2]
-                        nc.tensor.transpose(bank[:, u, P * a : P * (a + 1)], words, ident_f[:])
-                src = bank[:].rearrange("p u n -> p n u")
-                if c % 2 == 0:
-                    nc.vector.tensor_copy(out=gf[:, c % 4], in_=src)
-                else:
-                    nc.scalar.copy(out=gf[:, c % 4], in_=src)
-                if c % 2 == 0 and c >= 2:
-                    quant_x(c // 2 - 1)
-            quant_x(3)
-
-        prepare_x(xq, xs, 1)
-        prepare_x(yq, ys, 2)
+        for c in range(NC):
+            if c % 4 == 0:
+                xg.append(grpp.tile([P, 4, NW, 4], BF16, name="xg", tag="grp", align_bytes=64))
+            gf = xg[c // 4][:].bitcast(F32)
+            bank = tps.tile([P, 2, NW], F32, name="xb", tag="T")
+            for u in range(2):
+                for a in range(2):
+                    col = 256 * c + P * u
+                    nc.tensor.transpose(
+                        bank[:, u, P * a : P * (a + 1)],
+                        xr[a][:].bitcast(F32)[:, col : col + P],
+                        ident_f[:],
+                    )
+            src = bank[:].rearrange("p u n -> p n u")
+            if c % 2 == 0:
+                nc.vector.tensor_copy(out=gf[:, c % 4], in_=src)
+            else:
+                nc.scalar.copy(out=gf[:, c % 4], in_=src)
+            if c % 2 == 0 and c >= 2:
+                quant_x(c // 2 - 1)
+        quant_x(3)
         freed("u", 2)
 
         bt = tps.tile([P, P], BF16, name="bt", tag="T")
@@ -179,7 +176,7 @@ def tile_skconv2d_pa_kernel(tc, xw, S1s, U1s, U2s, S2s, bias, out):
                         col = 256 * (2 * b + c2) + P * u
                         nc.tensor.transpose(bank[:, c2, u, :], rf[:, col : col + P], ident_f[:])
                 src = bank[:].rearrange("p c u r -> p c r u")
-                if i >= 14 and b % 2 == 0:
+                if (b == 0 and i % 2 == 1) or (i >= 14 and b % 2 == 0):
                     nc.vector.tensor_copy(out=gf[:, 2 * b : 2 * b + 2], in_=src)
                 else:
                     nc.scalar.copy(out=gf[:, 2 * b : 2 * b + 2], in_=src)
@@ -197,7 +194,7 @@ def tile_skconv2d_pa_kernel(tc, xw, S1s, U1s, U2s, S2s, bias, out):
                     u2grp[i][:, sl].rearrange("p c r t -> p (c r t)"),
                 )
 
-        def first_stage(key, half, cod, scl, xc, xsc):
+        def first_stage(key, half, cod, scl):
             if half == 0 and key[0] == "u2":
                 hbank[key] = hps.tile([P, 2, NW], F32, name="hb", tag="h")
             elif half == 0:
@@ -208,8 +205,8 @@ def tile_skconv2d_pa_kernel(tc, xw, S1s, U1s, U2s, S2s, bias, out):
                     out=hb[:, half, :],
                     lhsT=cod[:, c, :].bitcast(FP8X4),
                     lhsT_scale=scl[:, c, :],
-                    rhs=xc[:, c, :].bitcast(FP8X4),
-                    rhs_scale=xsc[:, c, :],
+                    rhs=xq[:, c, :].bitcast(FP8X4),
+                    rhs_scale=xs[:, c, :],
                     start=(c == 0),
                     stop=(c == NC - 1),
                 )
@@ -286,25 +283,24 @@ def tile_skconv2d_pa_kernel(tc, xw, S1s, U1s, U2s, S2s, bias, out):
         quant_u2(1)
         for i in range(16):
             g, j = i // 4, i % 4
-            first_stage(("u2", i // 2), j % 2, u2cod[i][0], u2cod[i][1], xq, xs)
+            first_stage(("u2", i // 2), j % 2, u2cod[i][0], u2cod[i][1])
             if j % 2 == 1:
                 h_copy(g, j // 2, ("u2", i // 2))
             for pr in range(2):
                 if PAIR_ROUND[pr] == i:
                     for m in (2 * pr, 2 * pr + 1):
-                        first_stage(("s1", pr), m % 2, s1cod[m][0], s1cod[m][1], yq, ys)
+                        first_stage(("s1", pr), m % 2, s1cod[m][0], s1cod[m][1])
                     h_copy(4, pr, ("s1", pr))
             if i + 2 < 16:
                 transposes(i + 2)
-            if i == 15:
-                for s in (0, 1, 2, 4):
+            if i == S2_ROUND:
+                for s in range(3):
                     second_stage(s, s == 0, False)
             for t in range(8):
                 if S1_ROUND[t] == i:
                     s1_regroup(t)
-            for m in range(4):
-                if Q1_ROUND[m] == i:
-                    s1_quant(m)
+                    if t % 2 == 1:
+                        s1_quant(t // 2)
             for s in (4, 0, 1, 2, 3):
                 if W_ROUND[s] + 1 == i:
                     w_quant(s)
@@ -312,12 +308,12 @@ def tile_skconv2d_pa_kernel(tc, xw, S1s, U1s, U2s, S2s, bias, out):
                     w_regroup(s)
             if j == 0 and i > 0:
                 h_quant(g - 1)
-            if i == PAIR_ROUND[1] + 1:
-                h_quant(4)
             if i + 2 < 16:
                 quant_u2(i + 2)
         h_quant(3)
-        second_stage(3, False, True)
+        second_stage(3, False, False)
+        h_quant(4)
+        second_stage(4, False, True)
 
         for q in range(4):
             if q % 2 == 0:

@@ -20,20 +20,6 @@ NW = 256
 D = 4096
 NC = 8
 HALF = 2048
-RAW_BUFS = 7
-S1_BUFS = 4
-S1_V = 6
-
-STREAM = (
-    ("u", 0), ("u", 1), ("u", 2), ("w", 4), ("u", 3), ("w", 0), ("w", 1), ("u", 4), ("w", 2),
-    ("u", 5), ("u", 6), ("u", 7), ("u", 8), ("w", 3), ("u", 9), ("u", 10), ("s", 0), ("s", 1),
-    ("u", 11), ("s", 2), ("u", 12), ("u", 13), ("s", 3), ("u", 14), ("s", 4), ("s", 5),
-    ("u", 15), ("s", 6), ("s", 7),
-)
-W_ROUND = {4: 1, 0: 2, 1: 3, 2: 4, 3: 8}
-S1_ROUND = (9, 9, 10, 12, 13, 13, 14, 14)
-PAIR_ROUND = (14, 15)
-S2_ROUND = 14
 
 
 def tile_skconv2d_pa_kernel(tc, xw, S1s, U1s, U2s, S2s, bias, out):
@@ -46,8 +32,7 @@ def tile_skconv2d_pa_kernel(tc, xw, S1s, U1s, U2s, S2s, bias, out):
 
     with ExitStack() as ctx:
         const = ctx.enter_context(tc.tile_pool(name="const", bufs=1))
-        rawp = ctx.enter_context(tc.tile_pool(name="rawp", bufs=RAW_BUFS))
-        s1rp = ctx.enter_context(tc.tile_pool(name="s1rp", bufs=S1_BUFS))
+        rawp = ctx.enter_context(tc.tile_pool(name="rawp", bufs=8))
         grpp = ctx.enter_context(tc.tile_pool(name="grpp", bufs=3))
         codp = ctx.enter_context(tc.tile_pool(name="codp", bufs=3))
         s1gp = ctx.enter_context(tc.tile_pool(name="s1gp", bufs=2))
@@ -87,38 +72,29 @@ def tile_skconv2d_pa_kernel(tc, xw, S1s, U1s, U2s, S2s, bias, out):
                 )
         u2raw = {}
         s1raw = {}
-        state = {"ptr": 0, "u": RAW_BUFS - 2, "s": S1_BUFS}
 
-        def pump():
-            while state["ptr"] < len(STREAM):
-                kind, n = STREAM[state["ptr"]]
-                if kind != "w" and state[kind] == 0:
-                    break
-                if kind == "u":
-                    t = rawp.tile([P, D], BF16, name="u2r", tag="raw")
-                    nc.sync.dma_start(out=t[:], in_=u2v[:, n // 4, n % 4, :])
-                    u2raw[n] = t
-                    state["u"] = state["u"] - 1
-                elif kind == "s":
-                    t = s1rp.tile([P, HALF], BF16, name="s1r", tag="s1r")
-                    for q in range(4):
-                        nc.sync.dma_start(
-                            out=t[:, 512 * q : 512 * (q + 1)].rearrange("p (a x) -> p a x", a=4),
-                            in_=s1v[:, n, 4 * q : 4 * (q + 1)],
-                        )
-                    s1raw[n] = t
-                    state["s"] = state["s"] - 1
-                elif n == 4:
-                    nc.sync.dma_start(out=u1r[:], in_=u1v)
-                else:
-                    nc.sync.dma_start(out=s2r[:, n], in_=s2v[:, n])
-                state["ptr"] = state["ptr"] + 1
+        def load_raw(n):
+            if n < 16:
+                t = rawp.tile([P, D], BF16, name="u2r", tag="raw")
+                nc.sync.dma_start(out=t[:], in_=u2v[:, n // 4, n % 4, :])
+                u2raw[n] = t
+            elif n < 20:
+                m = n - 16
+                t = rawp.tile([P, D], BF16, name="s1r", tag="raw")
+                for part in range(8):
+                    nc.sync.dma_start(
+                        out=t[:, 512 * part : 512 * (part + 1)].rearrange("p (a x) -> p a x", a=4),
+                        in_=s1v[:, 2 * m + part // 4, 4 * (part % 4) : 4 * (part % 4 + 1)],
+                    )
+                s1raw[m] = t
+            if n == 3:
+                nc.sync.dma_start(out=u1r[:], in_=u1v)
+            if n in (5, 7, 9, 11):
+                g = (n - 5) // 2
+                nc.sync.dma_start(out=s2r[:, g], in_=s2v[:, g])
 
-        def freed(kind, count):
-            state[kind] = state[kind] + count
-            pump()
-
-        pump()
+        for n in range(6):
+            load_raw(n)
 
         def quant(codes, scales, src):
             nc.vector.quantize_mx(out=codes.bitcast(FP8X4), scales=scales, in_=src)
@@ -153,7 +129,8 @@ def tile_skconv2d_pa_kernel(tc, xw, S1s, U1s, U2s, S2s, bias, out):
             if c % 2 == 0 and c >= 2:
                 quant_x(c // 2 - 1)
         quant_x(3)
-        freed("u", 2)
+        load_raw(6)
+        load_raw(7)
 
         bt = tps.tile([P, P], BF16, name="bt", tag="T")
         nc.tensor.transpose(bt[:], bz[:], ident_b[:])
@@ -176,11 +153,11 @@ def tile_skconv2d_pa_kernel(tc, xw, S1s, U1s, U2s, S2s, bias, out):
                         col = 256 * (2 * b + c2) + P * u
                         nc.tensor.transpose(bank[:, c2, u, :], rf[:, col : col + P], ident_f[:])
                 src = bank[:].rearrange("p c u r -> p c r u")
-                if (b == 0 and i % 2 == 1) or (i >= 14 and b % 2 == 0):
+                if b == 0 and i % 2 == 1:
                     nc.vector.tensor_copy(out=gf[:, 2 * b : 2 * b + 2], in_=src)
                 else:
                     nc.scalar.copy(out=gf[:, 2 * b : 2 * b + 2], in_=src)
-            freed("u", 1)
+            load_raw(8 + i)
 
         def quant_u2(i):
             cod = codp.tile([P, NC, P], U32, name="u2c", tag="u2c", align_bytes=64)
@@ -195,10 +172,8 @@ def tile_skconv2d_pa_kernel(tc, xw, S1s, U1s, U2s, S2s, bias, out):
                 )
 
         def first_stage(key, half, cod, scl):
-            if half == 0 and key[0] == "u2":
+            if half == 0:
                 hbank[key] = hps.tile([P, 2, NW], F32, name="hb", tag="h")
-            elif half == 0:
-                hbank[key] = tps.tile([P, 2, NW], F32, name="hb1", tag="T")
             hb = hbank[key]
             for c in range(NC):
                 nc.tensor.matmul_mx(
@@ -236,12 +211,31 @@ def tile_skconv2d_pa_kernel(tc, xw, S1s, U1s, U2s, S2s, bias, out):
         def w_quant(s):
             quant(wc[:, s, :], ws[:, s, :], wgrp[s][:].rearrange("p o t -> p (o t)"))
 
-        acc = []
+        w_order = {4: 4, 6: 0, 8: 1, 10: 2, 12: 3}
+
+        transposes(0)
+        quant_u2(0)
+        transposes(1)
+        quant_u2(1)
+        for i in range(16):
+            g, j = i // 4, i % 4
+            first_stage(("u2", i // 2), j % 2, u2cod[i][0], u2cod[i][1])
+            if i + 2 < 16:
+                transposes(i + 2)
+            if j % 2 == 1:
+                h_copy(g, j // 2, ("u2", i // 2))
+            if i + 2 < 16:
+                quant_u2(i + 2)
+            if j == 3:
+                h_quant(g)
+            if i in w_order:
+                w_regroup(w_order[i])
+            if i - 1 in w_order:
+                w_quant(w_order[i - 1])
+
+        acc = [tps.tile([P, 512], F32, name="acc%d" % q, tag="T") for q in range(4)]
 
         def second_stage(s, start, stop):
-            if start:
-                for q in range(4):
-                    acc.append(tps.tile([P, 512], F32, name="acc%d" % q, tag="T"))
             for q in range(4):
                 nc.tensor.matmul_mx(
                     out=acc[q][:, 0:NW],
@@ -253,65 +247,33 @@ def tile_skconv2d_pa_kernel(tc, xw, S1s, U1s, U2s, S2s, bias, out):
                     stop=stop,
                 )
 
-        s1grp = {}
-        s1cod = {}
+        for g in range(4):
+            second_stage(g, g == 0, False)
 
-        def s1_regroup(t):
-            m, t2 = t // 2, t % 2
-            if t2 == 0:
-                s1grp[m] = s1gp.tile([P, NC, 2, 64, 4], BF16, name="s1g", tag="s1g", align_bytes=64)
-            src = s1raw[t][:].rearrange("p (g t r) -> p g r t", g=NC, t=4, r=64)
-            nc.vector.tensor_copy(out=s1grp[m][:, 0:S1_V, t2], in_=src[:, 0:S1_V])
-            nc.scalar.copy(out=s1grp[m][:, S1_V:NC, t2], in_=src[:, S1_V:NC])
-            freed("s", 1)
-
-        def s1_quant(m):
+        for m in range(4):
+            s1g = s1gp.tile([P, NC, 2, 64, 4], BF16, name="s1g", tag="s1g", align_bytes=64)
             cod = s1cp.tile([P, NC, P], U32, name="s1c", tag="s1c", align_bytes=64)
             scl = s1cp.tile([P, NC, P], U8, name="s1s", tag="s1s", align_bytes=64)
-            s1cod[m] = (cod, scl)
-            for hf in range(2):
-                sl = slice(4 * hf, 4 * hf + 4)
+            for t2 in range(2):
+                src = s1raw[m][:, HALF * t2 : HALF * (t2 + 1)].rearrange(
+                    "p (g t r) -> p g r t", g=NC, t=4, r=64
+                )
+                if 2 * m + t2 < 7:
+                    nc.vector.tensor_copy(out=s1g[:, 0:4, t2], in_=src[:, 0:4])
+                    nc.scalar.copy(out=s1g[:, 4:8, t2], in_=src[:, 4:8])
+            step = 4 if m < 3 else 2
+            for c0 in range(0, NC, step):
+                sl = slice(c0, c0 + step)
+                if m == 3:
+                    nc.vector.tensor_copy(out=s1g[:, sl, 1], in_=src[:, sl])
                 quant(
                     cod[:, sl, :].rearrange("p c r -> p (c r)"),
                     scl[:, sl, :].rearrange("p c r -> p (c r)"),
-                    s1grp[m][:, sl].rearrange("p c a r t -> p (c a r t)"),
+                    s1g[:, sl].rearrange("p c a r t -> p (c a r t)"),
                 )
-
-        transposes(0)
-        quant_u2(0)
-        transposes(1)
-        quant_u2(1)
-        for i in range(16):
-            g, j = i // 4, i % 4
-            first_stage(("u2", i // 2), j % 2, u2cod[i][0], u2cod[i][1])
-            if j % 2 == 1:
-                h_copy(g, j // 2, ("u2", i // 2))
-            for pr in range(2):
-                if PAIR_ROUND[pr] == i:
-                    for m in (2 * pr, 2 * pr + 1):
-                        first_stage(("s1", pr), m % 2, s1cod[m][0], s1cod[m][1])
-                    h_copy(4, pr, ("s1", pr))
-            if i + 2 < 16:
-                transposes(i + 2)
-            if i == S2_ROUND:
-                for s in range(3):
-                    second_stage(s, s == 0, False)
-            for t in range(8):
-                if S1_ROUND[t] == i:
-                    s1_regroup(t)
-                    if t % 2 == 1:
-                        s1_quant(t // 2)
-            for s in (4, 0, 1, 2, 3):
-                if W_ROUND[s] + 1 == i:
-                    w_quant(s)
-                if W_ROUND[s] == i:
-                    w_regroup(s)
-            if j == 0 and i > 0:
-                h_quant(g - 1)
-            if i + 2 < 16:
-                quant_u2(i + 2)
-        h_quant(3)
-        second_stage(3, False, False)
+            first_stage(("s1", m // 2), m % 2, cod, scl)
+            if m % 2 == 1:
+                h_copy(4, m // 2, ("s1", m // 2))
         h_quant(4)
         second_stage(4, False, True)
 

from contextlib import ExitStack

import concourse.mybir as mybir
from concourse.masks import make_identity

PIN = True

FLOPS = 2 * 256 * 4096 * (512 + 2048) + 2 * 256 * 512 * (512 + 2048)

BF16 = mybir.dt.bfloat16
F32 = mybir.dt.float32
U32 = mybir.dt.uint32
U8 = mybir.dt.uint8
FP8X4 = mybir.dt.float8_e4m3fn_x4
ACT = mybir.ActivationFunctionType
ALU = mybir.AluOpType

P = 128
NW = 256
D = 4096
NC = 8
HALF = 2048


def tile_skconv2d_pa_kernel(tc, xw, S1s, U1s, U2s, S2s, bias, out):
    nc = tc.nc
    u2v = U2s.rearrange("t r k -> (t r) k").rearrange("(g p j) k -> p g j k", p=P, j=4)
    s1v = S1s.rearrange("t (a p e) r -> p t a (e r)", a=16, p=P, e=2)
    u1v = U1s.rearrange("t r o -> (t r) o").rearrange("(j p) o -> p j o", p=P)
    s2v = S2s.rearrange("t r o -> (t r) o").rearrange("(g p j) o -> p g j o", p=P, j=4)
    outv = out.rearrange("b (q p) i j -> p q b (i j)", p=P)

    with ExitStack() as ctx:
        const = ctx.enter_context(tc.tile_pool(name="const", bufs=1))
        rawp = ctx.enter_context(tc.tile_pool(name="rawp", bufs=8))
        grpp = ctx.enter_context(tc.tile_pool(name="grpp", bufs=3))
        codp = ctx.enter_context(tc.tile_pool(name="codp", bufs=3))
        s1gp = ctx.enter_context(tc.tile_pool(name="s1gp", bufs=2))
        s1cp = ctx.enter_context(tc.tile_pool(name="s1cp", bufs=4))
        wgp = ctx.enter_context(tc.tile_pool(name="wgp", bufs=2))
        hgp = ctx.enter_context(tc.tile_pool(name="hgp", bufs=2))
        tps = ctx.enter_context(tc.psum_pool(name="tps", bufs=6))
        hps = ctx.enter_context(tc.psum_pool(name="hps", bufs=2))
        if PIN:
            ctx.enter_context(tc.manual_schedule())

        ident_f = const.tile([P, P], F32, name="ident_f")
        make_identity(nc, ident_f[:])
        ident_b = const.tile([P, P], BF16, name="ident_b")
        make_identity(nc, ident_b[:])
        bz = const.tile([P, P], BF16, name="bz")
        nc.vector.memset(bz[:], 0.0)
        nc.scalar.dma_start(out=bz[0:4, :], in_=bias.rearrange("(a c) -> a c", a=4))

        xq = const.tile([P, NC, NW], U32, name="xq", align_bytes=64)
        xs = const.tile([P, NC, NW], U8, name="xs", align_bytes=64)
        s2r = const.tile([P, 4, 4, 512], BF16, name="s2r")
        u1r = const.tile([P, 4, 512], BF16, name="u1r")
        wc = const.tile([P, 5, 512], U32, name="wc", align_bytes=64)
        ws = const.tile([P, 5, 512], U8, name="ws", align_bytes=64)
        hqc = const.tile([P, 5, NW], U32, name="hqc", align_bytes=64)
        hqs = const.tile([P, 5, NW], U8, name="hqs", align_bytes=64)
        osb = const.tile([P, 4, NW], F32, name="osb")
        b2 = const.tile([P, 4], F32, name="b2")

        xr = [rawp.tile([P, D], BF16, name="xr%d" % a, tag="raw") for a in range(2)]
        for hf in range(2):
            for a in range(2):
                nc.sync.dma_start(
                    out=xr[a][:, HALF * hf : HALF * (hf + 1)],
                    in_=xw[P * a : P * (a + 1), HALF * hf : HALF * (hf + 1)],
                )
        u2raw = {}
        s1raw = {}

        def load_raw(n):
            if n < 16:
                t = rawp.tile([P, D], BF16, name="u2r", tag="raw")
                nc.sync.dma_start(out=t[:], in_=u2v[:, n // 4, n % 4, :])
                u2raw[n] = t
            elif n < 20:
                m = n - 16
                t = rawp.tile([P, D], BF16, name="s1r", tag="raw")
                for part in range(8):
                    nc.sync.dma_start(
                        out=t[:, 512 * part : 512 * (part + 1)].rearrange("p (a x) -> p a x", a=4),
                        in_=s1v[:, 2 * m + part // 4, 4 * (part % 4) : 4 * (part % 4 + 1)],
                    )
                s1raw[m] = t
            if n == 3:
                nc.sync.dma_start(out=u1r[:], in_=u1v)
            if n in (5, 7, 9, 11):
                g = (n - 5) // 2
                nc.sync.dma_start(out=s2r[:, g], in_=s2v[:, g])

        for n in range(6):
            load_raw(n)

        def quant(codes, scales, src):
            nc.vector.quantize_mx(out=codes.bitcast(FP8X4), scales=scales, in_=src)

        xg = []

        def quant_x(k):
            quant(
                xq[:, 2 * k : 2 * k + 2, :].rearrange("p c n -> p (c n)"),
                xs[:, 2 * k : 2 * k + 2, :].rearrange("p c n -> p (c n)"),
                xg[k // 2][:, 2 * (k % 2) : 2 * (k % 2) + 2].rearrange("p c n t -> p (c n t)"),
            )

        for c in range(NC):
            if c % 4 == 0:
                xg.append(grpp.tile([P, 4, NW, 4], BF16, name="xg", tag="grp", align_bytes=64))
            gf = xg[c // 4][:].bitcast(F32)
            bank = tps.tile([P, 2, NW], F32, name="xb", tag="T")
            for u in range(2):
                for a in range(2):
                    col = 256 * c + P * u
                    nc.tensor.transpose(
                        bank[:, u, P * a : P * (a + 1)],
                        xr[a][:].bitcast(F32)[:, col : col + P],
                        ident_f[:],
                    )
            src = bank[:].rearrange("p u n -> p n u")
            if c % 2 == 0:
                nc.vector.tensor_copy(out=gf[:, c % 4], in_=src)
            else:
                nc.scalar.copy(out=gf[:, c % 4], in_=src)
            if c % 2 == 0 and c >= 2:
                quant_x(c // 2 - 1)
        quant_x(3)
        load_raw(6)
        load_raw(7)

        bt = tps.tile([P, P], BF16, name="bt", tag="T")
        nc.tensor.transpose(bt[:], bz[:], ident_b[:])
        nc.scalar.mul(b2[:], bt[:, 0:4], 2.0)

        u2grp = {}
        u2cod = {}
        hbank = {}
        hgrp = {}

        def transposes(i):
            grp = grpp.tile([P, NC, P, 4], BF16, name="u2g", tag="grp", align_bytes=64)
            u2grp[i] = grp
            gf = grp[:].bitcast(F32)
            rf = u2raw[i][:].bitcast(F32)
            for b in range(4):
                bank = tps.tile([P, 2, 2, P], F32, name="ub", tag="T")
                for c2 in range(2):
                    for u in range(2):
                        col = 256 * (2 * b + c2) + P * u
                        nc.tensor.transpose(bank[:, c2, u, :], rf[:, col : col + P], ident_f[:])
                src = bank[:].rearrange("p c u r -> p c r u")
                if b == 0 and i % 2 == 1:
                    nc.vector.tensor_copy(out=gf[:, 2 * b : 2 * b + 2], in_=src)
                else:
                    nc.scalar.copy(out=gf[:, 2 * b : 2 * b + 2], in_=src)
            load_raw(8 + i)

        def quant_u2(i):
            cod = codp.tile([P, NC, P], U32, name="u2c", tag="u2c", align_bytes=64)
            scl = codp.tile([P, NC, P], U8, name="u2s", tag="u2s", align_bytes=64)
            u2cod[i] = (cod, scl)
            for hf in range(2):
                sl = slice(4 * hf, 4 * hf + 4)
                quant(
                    cod[:, sl, :].rearrange("p c r -> p (c r)"),
                    scl[:, sl, :].rearrange("p c r -> p (c r)"),
                    u2grp[i][:, sl].rearrange("p c r t -> p (c r t)"),
                )

        def first_stage(key, half, cod, scl):
            if half == 0:
                hbank[key] = hps.tile([P, 2, NW], F32, name="hb", tag="h")
            hb = hbank[key]
            for c in range(NC):
                nc.tensor.matmul_mx(
                    out=hb[:, half, :],
                    lhsT=cod[:, c, :].bitcast(FP8X4),
                    lhsT_scale=scl[:, c, :],
                    rhs=xq[:, c, :].bitcast(FP8X4),
                    rhs_scale=xs[:, c, :],
                    start=(c == 0),
                    stop=(c == NC - 1),
                )

        def h_copy(s, pair, key):
            if pair == 0:
                hgrp[s] = hgp.tile([P, NW, 4], BF16, name="hg", tag="hg", align_bytes=64)
            nc.scalar.copy(
                out=hgrp[s][:, :, 2 * pair : 2 * pair + 2],
                in_=hbank[key][:].rearrange("p j n -> p n j"),
            )

        def h_quant(s):
            quant(hqc[:, s, :], hqs[:, s, :], hgrp[s][:].rearrange("p n t -> p (n t)"))

        wgrp = {}

        def w_regroup(s):
            wg = wgp.tile([P, 512, 4], BF16, name="wg", tag="wg", align_bytes=64)
            wgrp[s] = wg
            src = u1r[:] if s == 4 else s2r[:, s]
            nc.vector.tensor_copy(
                out=wg[:].rearrange("p (c i) t -> p c t i", i=4),
                in_=src.rearrange("p t (c i) -> p c t i", i=4),
            )

        def w_quant(s):
            quant(wc[:, s, :], ws[:, s, :], wgrp[s][:].rearrange("p o t -> p (o t)"))

        w_order = {4: 4, 6: 0, 8: 1, 10: 2, 12: 3}

        transposes(0)
        quant_u2(0)
        transposes(1)
        quant_u2(1)
        for i in range(16):
            g, j = i // 4, i % 4
            first_stage(("u2", i // 2), j % 2, u2cod[i][0], u2cod[i][1])
            if i + 2 < 16:
                transposes(i + 2)
            if j % 2 == 1:
                h_copy(g, j // 2, ("u2", i // 2))
            if i + 2 < 16:
                quant_u2(i + 2)
            if j == 3:
                h_quant(g)
            if i in w_order:
                w_regroup(w_order[i])
            if i - 1 in w_order:
                w_quant(w_order[i - 1])

        acc = [tps.tile([P, 512], F32, name="acc%d" % q, tag="T") for q in range(4)]

        def second_stage(s, start, stop):
            for q in range(4):
                nc.tensor.matmul_mx(
                    out=acc[q][:, 0:NW],
                    lhsT=wc[:, s, P * q : P * (q + 1)].bitcast(FP8X4),
                    lhsT_scale=ws[:, s, P * q : P * (q + 1)],
                    rhs=hqc[:, s, :].bitcast(FP8X4),
                    rhs_scale=hqs[:, s, :],
                    start=start,
                    stop=stop,
                )

        for g in range(4):
            second_stage(g, g == 0, False)

        for m in range(4):
            s1g = s1gp.tile([P, NC, 2, 64, 4], BF16, name="s1g", tag="s1g", align_bytes=64)
            cod = s1cp.tile([P, NC, P], U32, name="s1c", tag="s1c", align_bytes=64)
            scl = s1cp.tile([P, NC, P], U8, name="s1s", tag="s1s", align_bytes=64)
            for t2 in range(2):
                src = s1raw[m][:, HALF * t2 : HALF * (t2 + 1)].rearrange(
                    "p (g t r) -> p g r t", g=NC, t=4, r=64
                )
                if 2 * m + t2 < 7:
                    nc.vector.tensor_copy(out=s1g[:, 0:4, t2], in_=src[:, 0:4])
                    nc.scalar.copy(out=s1g[:, 4:8, t2], in_=src[:, 4:8])
            step = 4 if m < 3 else 2
            for c0 in range(0, NC, step):
                sl = slice(c0, c0 + step)
                if m == 3:
                    nc.vector.tensor_copy(out=s1g[:, sl, 1], in_=src[:, sl])
                quant(
                    cod[:, sl, :].rearrange("p c r -> p (c r)"),
                    scl[:, sl, :].rearrange("p c r -> p (c r)"),
                    s1g[:, sl].rearrange("p c a r t -> p (c a r t)"),
                )
            first_stage(("s1", m // 2), m % 2, cod, scl)
            if m % 2 == 1:
                h_copy(4, m // 2, ("s1", m // 2))
        h_quant(4)
        second_stage(4, False, True)

        for q in range(4):
            if q % 2 == 0:
                nc.scalar.activation(
                    out=osb[:, q, :], in_=acc[q][:, 0:NW], func=ACT.Identity,
                    bias=b2[:, q : q + 1], scale=0.125,
                )
            else:
                nc.vector.tensor_scalar(
                    out=osb[:, q, :], in0=acc[q][:, 0:NW], scalar1=0.125,
                    scalar2=b2[:, q : q + 1], op0=ALU.mult, op1=ALU.add,
                )
            nc.sync.dma_start(out=outv[:, q], in_=osb[:, q, :].rearrange("p (b s) -> p b s", b=4))
